import numpy as np
import ml_dtypes

BF16 = ml_dtypes.bfloat16


def bf(x):
    return np.asarray(x, np.float32).astype(BF16)


def f32(x):
    return np.asarray(x, np.float32)


def f64(x):
    return np.asarray(x).astype(np.float64)


def striped(idx):
    return np.tile(idx.reshape(-1, 16).T, (8, 1))


C, S, N, T = 256, 768, 384, 768


def setup_inputs():
    return {"base": f32(np.random.standard_normal((C, S))), "xs": bf(np.random.standard_normal((C, T))), "w1": bf(np.random.standard_normal((C, C)) / np.sqrt(C)), "b1": f32(0.1 * np.random.standard_normal((C, 1))), "w2": bf(np.random.standard_normal((C, C)) * np.sqrt(2.0 / C)), "b2": f32(0.1 * np.random.standard_normal((C, 1))), "offs": striped(np.random.permutation(S)[:N])}


def reference(base, xs, w1, b1, w2, b2, offs):
    idx = offs[:16].T.reshape(-1)
    h = np.maximum(f64(w1).T @ f64(xs) + f64(b1), 0.0)
    y = f64(w2).T @ h + f64(b2)
    out = f64(base).copy()
    out[:, idx] = y[:, :N] + y[:, N:]
    return out

@@ -1,0 +1,81 @@
+import concourse.mybir as mybir
+
+BF16, F32, U16 = mybir.dt.bfloat16, mybir.dt.float32, mybir.dt.uint16
+ADD, MAX = mybir.AluOpType.add, mybir.AluOpType.max
+RELU = mybir.ActivationFunctionType.Relu
+IDENTITY = mybir.ActivationFunctionType.Identity
+
+P = 128
+C = 256
+S = 768
+N = 384
+BLOCKS = C // P
+HALVES = 2
+
+FLOPS = 2 * (2 * C * C * HALVES * N)
+
+
+def tile_inter_classifier_kernel(tc, base, xs, w1, b1, w2, b2, offs, out):
+    nc = tc.nc
+    with (
+        tc.tile_pool(name="held", bufs=1) as held,
+        tc.psum_pool(name="psum", bufs=BLOCKS * HALVES) as psum,
+    ):
+        xs_sb = [held.tile([P, HALVES * N], BF16, name=f"xs_sb{d}") for d in range(BLOCKS)]
+        w1_sb = [held.tile([P, C], BF16, name=f"w1_sb{d}") for d in range(BLOCKS)]
+        w2_sb = [held.tile([P, C], BF16, name=f"w2_sb{k}") for k in range(BLOCKS)]
+        window = [held.tile([P, S], F32, name=f"window{c}") for c in range(BLOCKS)]
+        offsets = held.tile([P, N // 16], U16, name="offsets")
+        b1_sb = held.tile([P, BLOCKS], F32, name="b1_sb")
+        b2_sb = held.tile([P, BLOCKS], F32, name="b2_sb")
+
+        for d in range(BLOCKS):
+            nc.sync.dma_start(xs_sb[d][:], xs[d * P : (d + 1) * P, :])
+            nc.scalar.dma_start(w1_sb[d][:], w1[d * P : (d + 1) * P, :])
+        with nc.allow_non_contiguous_dma(reason="one float32 of a bias to each partition"):
+            nc.scalar.dma_start(b1_sb[:], b1.rearrange("(k p) o -> p (k o)", p=P))
+        for k in range(BLOCKS):
+            nc.scalar.dma_start(w2_sb[k][:], w2[k * P : (k + 1) * P, :])
+        with nc.allow_non_contiguous_dma(reason="one float32 of a bias to each partition"):
+            nc.scalar.dma_start(b2_sb[:], b2.rearrange("(c p) o -> p (c o)", p=P))
+        nc.sync.dma_start(offsets[:], offs)
+        for c in range(BLOCKS):
+            nc.sync.dma_start(window[c][:], base[c * P : (c + 1) * P, :])
+
+        h_sb = [[None] * HALVES for k in range(BLOCKS)]
+        for half in range(HALVES):
+            tokens = slice(half * N, (half + 1) * N)
+            for k in range(BLOCKS):
+                h_ps = psum.tile([P, N], F32, name="h_ps")
+                for d in range(BLOCKS):
+                    nc.tensor.matmul(
+                        h_ps[:],
+                        w1_sb[d][:, k * P : (k + 1) * P],
+                        xs_sb[d][:, tokens],
+                        start=(d == 0),
+                        stop=(d == BLOCKS - 1),
+                    )
+                h_sb[k][half] = held.tile([P, N], BF16, name=f"h_sb{k}_{half}")
+                if k == 0:
+                    nc.scalar.activation(h_sb[k][half][:], h_ps[:], RELU, bias=b1_sb[:, k : k + 1])
+                else:
+                    nc.vector.tensor_scalar(h_sb[k][half][:], h_ps[:], b1_sb[:, k : k + 1], 0.0, ADD, MAX)
+
+        y_sb = [[None] * HALVES for c in range(BLOCKS)]
+        for half in range(HALVES):
+            for c in range(BLOCKS):
+                y_ps = psum.tile([P, N], F32, name="y_ps")
+                for k in range(BLOCKS):
+                    nc.tensor.matmul(
+                        y_ps[:],
+                        w2_sb[k][:, c * P : (c + 1) * P],
+                        h_sb[k][half][:],
+                        start=(k == 0),
+                        stop=(k == BLOCKS - 1),
+                    )
+                y_sb[c][half] = held.tile([P, N], F32, name=f"y_sb{c}_{half}")
+                nc.scalar.activation(y_sb[c][half][:], y_ps[:], IDENTITY, bias=b2_sb[:, c : c + 1])
+
+        for c in range(BLOCKS):
+            nc.vector.tensor_tensor(window[c][:].indirect(offsets[:]), y_sb[c][0][:], y_sb[c][1][:], ADD)
+            nc.sync.dma_start(out[c * P : (c + 1) * P, :], window[c][:])

@@ -62,8 +62,8 @@ def tile_inter_classifier_kernel(tc, base, xs, w1, b1, w2, b2, offs, out):
                     nc.vector.tensor_scalar(h_sb[k][half][:], h_ps[:], b1_sb[:, k : k + 1], 0.0, ADD, MAX)
 
         y_sb = [[None] * HALVES for c in range(BLOCKS)]
-        for half in range(HALVES):
-            for c in range(BLOCKS):
+        for c in range(BLOCKS):
+            for half in range(HALVES):
                 y_ps = psum.tile([P, N], F32, name="y_ps")
                 for k in range(BLOCKS):
                     nc.tensor.matmul(
@@ -76,6 +76,5 @@ def tile_inter_classifier_kernel(tc, base, xs, w1, b1, w2, b2, offs, out):
                 y_sb[c][half] = held.tile([P, N], F32, name=f"y_sb{c}_{half}")
                 nc.scalar.activation(y_sb[c][half][:], y_ps[:], IDENTITY, bias=b2_sb[:, c : c + 1])
 
-        for c in range(BLOCKS):
             nc.vector.tensor_tensor(window[c][:].indirect(offsets[:]), y_sb[c][0][:], y_sb[c][1][:], ADD)
             nc.sync.dma_start(out[c * P : (c + 1) * P, :], window[c][:])

@@ -29,18 +29,19 @@ def tile_inter_classifier_kernel(tc, base, xs, w1, b1, w2, b2, offs, out):
         b1_sb = held.tile([P, BLOCKS], F32, name="b1_sb")
         b2_sb = held.tile([P, BLOCKS], F32, name="b2_sb")
 
-        for d in range(BLOCKS):
-            nc.sync.dma_start(xs_sb[d][:], xs[d * P : (d + 1) * P, :])
-            nc.scalar.dma_start(w1_sb[d][:], w1[d * P : (d + 1) * P, :])
+        queues = (nc.sync, nc.scalar)
         with nc.allow_non_contiguous_dma(reason="one float32 of a bias to each partition"):
-            nc.scalar.dma_start(b1_sb[:], b1.rearrange("(k p) o -> p (k o)", p=P))
-        for k in range(BLOCKS):
-            nc.scalar.dma_start(w2_sb[k][:], w2[k * P : (k + 1) * P, :])
-        with nc.allow_non_contiguous_dma(reason="one float32 of a bias to each partition"):
-            nc.scalar.dma_start(b2_sb[:], b2.rearrange("(c p) o -> p (c o)", p=P))
+            nc.gpsimd.dma_start(b1_sb[:], b1.rearrange("(k p) o -> p (k o)", p=P))
+            nc.gpsimd.dma_start(b2_sb[:], b2.rearrange("(c p) o -> p (c o)", p=P))
+        for block in range(BLOCKS):
+            rows = slice(block * P, (block + 1) * P)
+            queues[block].dma_start(w1_sb[block][:], w1[rows, :])
+            queues[block].dma_start(xs_sb[block][:], xs[rows, :])
         nc.sync.dma_start(offsets[:], offs)
-        for c in range(BLOCKS):
-            nc.sync.dma_start(window[c][:], base[c * P : (c + 1) * P, :])
+        for block in range(BLOCKS):
+            rows = slice(block * P, (block + 1) * P)
+            queues[block].dma_start(w2_sb[block][:], w2[rows, :])
+            queues[block].dma_start(window[block][:], base[rows, :])
 
         h_sb = [[None] * HALVES for k in range(BLOCKS)]
         for half in range(HALVES):

@@ -12,6 +12,8 @@ N = 384
 BLOCKS = C // P
 HALVES = 2
 
+WARM_MATMULS = 16
+
 FLOPS = 2 * (2 * C * C * HALVES * N)
 
 
@@ -29,19 +31,24 @@ def tile_inter_classifier_kernel(tc, base, xs, w1, b1, w2, b2, offs, out):
         b1_sb = held.tile([P, BLOCKS], F32, name="b1_sb")
         b2_sb = held.tile([P, BLOCKS], F32, name="b2_sb")
 
-        queues = (nc.sync, nc.scalar)
+        for d in range(BLOCKS):
+            nc.sync.dma_start(xs_sb[d][:], xs[d * P : (d + 1) * P, :])
+            nc.scalar.dma_start(w1_sb[d][:], w1[d * P : (d + 1) * P, :])
         with nc.allow_non_contiguous_dma(reason="one float32 of a bias to each partition"):
-            nc.gpsimd.dma_start(b1_sb[:], b1.rearrange("(k p) o -> p (k o)", p=P))
-            nc.gpsimd.dma_start(b2_sb[:], b2.rearrange("(c p) o -> p (c o)", p=P))
-        for block in range(BLOCKS):
-            rows = slice(block * P, (block + 1) * P)
-            queues[block].dma_start(w1_sb[block][:], w1[rows, :])
-            queues[block].dma_start(xs_sb[block][:], xs[rows, :])
+            nc.scalar.dma_start(b1_sb[:], b1.rearrange("(k p) o -> p (k o)", p=P))
+        for k in range(BLOCKS):
+            nc.scalar.dma_start(w2_sb[k][:], w2[k * P : (k + 1) * P, :])
+        with nc.allow_non_contiguous_dma(reason="one float32 of a bias to each partition"):
+            nc.scalar.dma_start(b2_sb[:], b2.rearrange("(c p) o -> p (c o)", p=P))
         nc.sync.dma_start(offsets[:], offs)
-        for block in range(BLOCKS):
-            rows = slice(block * P, (block + 1) * P)
-            queues[block].dma_start(w2_sb[block][:], w2[rows, :])
-            queues[block].dma_start(window[block][:], base[rows, :])
+        for c in range(BLOCKS):
+            nc.sync.dma_start(window[c][:], base[c * P : (c + 1) * P, :])
+
+        zeros = held.tile([P, P], BF16, name="zeros")
+        nc.vector.memset(zeros[:], 0.0)
+        warm_ps = psum.tile([P, P], F32, name="warm_ps", tag="y_ps")
+        for i in range(WARM_MATMULS):
+            nc.tensor.matmul(warm_ps[:], zeros[:], zeros[:], start=True, stop=True)
 
         h_sb = [[None] * HALVES for k in range(BLOCKS)]
         for half in range(HALVES):

@@ -50,6 +50,9 @@ def tile_inter_classifier_kernel(tc, base, xs, w1, b1, w2, b2, offs, out):
         for i in range(WARM_MATMULS):
             nc.tensor.matmul(warm_ps[:], zeros[:], zeros[:], start=True, stop=True)
 
+        table_warmer = held.tile([P, 1], F32, name="table_warmer")
+        nc.scalar.activation(table_warmer[:], zeros[:, 0:1], RELU)
+
         h_sb = [[None] * HALVES for k in range(BLOCKS)]
         for half in range(HALVES):
             tokens = slice(half * N, (half + 1) * N)

@@ -23,23 +23,23 @@ def tile_inter_classifier_kernel(tc, base, xs, w1, b1, w2, b2, offs, out):
         tc.tile_pool(name="held", bufs=1) as held,
         tc.psum_pool(name="psum", bufs=BLOCKS * HALVES) as psum,
     ):
-        xs_sb = [held.tile([P, HALVES * N], BF16, name=f"xs_sb{d}") for d in range(BLOCKS)]
-        w1_sb = [held.tile([P, C], BF16, name=f"w1_sb{d}") for d in range(BLOCKS)]
-        w2_sb = [held.tile([P, C], BF16, name=f"w2_sb{k}") for k in range(BLOCKS)]
-        window = [held.tile([P, S], F32, name=f"window{c}") for c in range(BLOCKS)]
-        offsets = held.tile([P, N // 16], U16, name="offsets")
+        xs_sb = [held.tile([P, BLOCKS, N], BF16, name=f"xs_sb{half}") for half in range(HALVES)]
+        w1_sb = held.tile([P, BLOCKS, C], BF16, name="w1_sb")
+        w2_sb = held.tile([P, BLOCKS, C], BF16, name="w2_sb")
         b1_sb = held.tile([P, BLOCKS], F32, name="b1_sb")
         b2_sb = held.tile([P, BLOCKS], F32, name="b2_sb")
+        offsets = held.tile([P, N // 16], U16, name="offsets")
+        window = [held.tile([P, S], F32, name=f"window{c}") for c in range(BLOCKS)]
 
-        for d in range(BLOCKS):
-            nc.sync.dma_start(xs_sb[d][:], xs[d * P : (d + 1) * P, :])
-            nc.scalar.dma_start(w1_sb[d][:], w1[d * P : (d + 1) * P, :])
+        xs_blocks = xs.rearrange("(d p) t -> p d t", p=P)
+        for half in range(HALVES):
+            nc.sync.dma_start(xs_sb[half][:], xs_blocks[:, :, half * N : (half + 1) * N])
+        nc.scalar.dma_start(w1_sb[:], w1.rearrange("(d p) k -> p d k", p=P))
         with nc.allow_non_contiguous_dma(reason="one float32 of a bias to each partition"):
             nc.scalar.dma_start(b1_sb[:], b1.rearrange("(k p) o -> p (k o)", p=P))
-        for k in range(BLOCKS):
-            nc.scalar.dma_start(w2_sb[k][:], w2[k * P : (k + 1) * P, :])
+        nc.sync.dma_start(w2_sb[:], w2.rearrange("(k p) c -> p k c", p=P))
         with nc.allow_non_contiguous_dma(reason="one float32 of a bias to each partition"):
-            nc.scalar.dma_start(b2_sb[:], b2.rearrange("(c p) o -> p (c o)", p=P))
+            nc.sync.dma_start(b2_sb[:], b2.rearrange("(c p) o -> p (c o)", p=P))
         nc.sync.dma_start(offsets[:], offs)
         for c in range(BLOCKS):
             nc.sync.dma_start(window[c][:], base[c * P : (c + 1) * P, :])
@@ -55,14 +55,13 @@ def tile_inter_classifier_kernel(tc, base, xs, w1, b1, w2, b2, offs, out):
 
         h_sb = [[None] * HALVES for k in range(BLOCKS)]
         for half in range(HALVES):
-            tokens = slice(half * N, (half + 1) * N)
             for k in range(BLOCKS):
                 h_ps = psum.tile([P, N], F32, name="h_ps")
                 for d in range(BLOCKS):
                     nc.tensor.matmul(
                         h_ps[:],
-                        w1_sb[d][:, k * P : (k + 1) * P],
-                        xs_sb[d][:, tokens],
+                        w1_sb[:, d, k * P : (k + 1) * P],
+                        xs_sb[half][:, d, :],
                         start=(d == 0),
                         stop=(d == BLOCKS - 1),
                     )
@@ -79,7 +78,7 @@ def tile_inter_classifier_kernel(tc, base, xs, w1, b1, w2, b2, offs, out):
                 for k in range(BLOCKS):
                     nc.tensor.matmul(
                         y_ps[:],
-                        w2_sb[k][:, c * P : (c + 1) * P],
+                        w2_sb[:, k, c * P : (c + 1) * P],
                         h_sb[k][half][:],
                         start=(k == 0),
                         stop=(k == BLOCKS - 1),

@@ -23,20 +23,23 @@ def tile_inter_classifier_kernel(tc, base, xs, w1, b1, w2, b2, offs, out):
         tc.tile_pool(name="held", bufs=1) as held,
         tc.psum_pool(name="psum", bufs=BLOCKS * HALVES) as psum,
     ):
-        xs_sb = [held.tile([P, BLOCKS, N], BF16, name=f"xs_sb{half}") for half in range(HALVES)]
-        w1_sb = held.tile([P, BLOCKS, C], BF16, name="w1_sb")
+        xs_sb = [
+            [held.tile([P, N], BF16, name=f"xs_sb{half}_{d}") for d in range(BLOCKS)] for half in range(HALVES)
+        ]
+        w1_sb = [held.tile([P, C], BF16, name=f"w1_sb{d}") for d in range(BLOCKS)]
         w2_sb = held.tile([P, BLOCKS, C], BF16, name="w2_sb")
         b1_sb = held.tile([P, BLOCKS], F32, name="b1_sb")
         b2_sb = held.tile([P, BLOCKS], F32, name="b2_sb")
         offsets = held.tile([P, N // 16], U16, name="offsets")
         window = [held.tile([P, S], F32, name=f"window{c}") for c in range(BLOCKS)]
 
-        xs_blocks = xs.rearrange("(d p) t -> p d t", p=P)
-        for half in range(HALVES):
-            nc.sync.dma_start(xs_sb[half][:], xs_blocks[:, :, half * N : (half + 1) * N])
-        nc.scalar.dma_start(w1_sb[:], w1.rearrange("(d p) k -> p d k", p=P))
+        for d in range(BLOCKS):
+            nc.scalar.dma_start(w1_sb[d][:], w1[d * P : (d + 1) * P, :])
         with nc.allow_non_contiguous_dma(reason="one float32 of a bias to each partition"):
             nc.scalar.dma_start(b1_sb[:], b1.rearrange("(k p) o -> p (k o)", p=P))
+        for half in range(HALVES):
+            for d in range(BLOCKS):
+                nc.sync.dma_start(xs_sb[half][d][:], xs[d * P : (d + 1) * P, half * N : (half + 1) * N])
         nc.sync.dma_start(w2_sb[:], w2.rearrange("(k p) c -> p k c", p=P))
         with nc.allow_non_contiguous_dma(reason="one float32 of a bias to each partition"):
             nc.sync.dma_start(b2_sb[:], b2.rearrange("(c p) o -> p (c o)", p=P))
@@ -55,21 +58,22 @@ def tile_inter_classifier_kernel(tc, base, xs, w1, b1, w2, b2, offs, out):
 
         h_sb = [[None] * HALVES for k in range(BLOCKS)]
         for half in range(HALVES):
-            for k in range(BLOCKS):
-                h_ps = psum.tile([P, N], F32, name="h_ps")
-                for d in range(BLOCKS):
+            h_ps = [psum.tile([P, N], F32, name=f"h_ps{k}", tag="h_ps") for k in range(BLOCKS)]
+            for d in range(BLOCKS):
+                for k in range(BLOCKS):
                     nc.tensor.matmul(
-                        h_ps[:],
-                        w1_sb[:, d, k * P : (k + 1) * P],
-                        xs_sb[half][:, d, :],
+                        h_ps[k][:],
+                        w1_sb[d][:, k * P : (k + 1) * P],
+                        xs_sb[half][d][:],
                         start=(d == 0),
                         stop=(d == BLOCKS - 1),
                     )
+            for k in range(BLOCKS):
                 h_sb[k][half] = held.tile([P, N], BF16, name=f"h_sb{k}_{half}")
                 if k == 0:
-                    nc.scalar.activation(h_sb[k][half][:], h_ps[:], RELU, bias=b1_sb[:, k : k + 1])
+                    nc.scalar.activation(h_sb[k][half][:], h_ps[k][:], RELU, bias=b1_sb[:, k : k + 1])
                 else:
-                    nc.vector.tensor_scalar(h_sb[k][half][:], h_ps[:], b1_sb[:, k : k + 1], 0.0, ADD, MAX)
+                    nc.vector.tensor_scalar(h_sb[k][half][:], h_ps[k][:], b1_sb[:, k : k + 1], 0.0, ADD, MAX)
 
         y_sb = [[None] * HALVES for c in range(BLOCKS)]
         for c in range(BLOCKS):

@@ -12,7 +12,7 @@ N = 384
 BLOCKS = C // P
 HALVES = 2
 
-WARM_MATMULS = 16
+WARM_MATMULS = 10
 
 FLOPS = 2 * (2 * C * C * HALVES * N)
 

@@ -9,24 +9,28 @@ P = 128
 C = 256
 S = 768
 N = 384
+T = 2 * N
 BLOCKS = C // P
+
 HALVES = 2
+
+CHUNK_WIDTHS = (384, 192, 192)
+CHUNKS = [slice(sum(CHUNK_WIDTHS[:i]), sum(CHUNK_WIDTHS[: i + 1])) for i in range(len(CHUNK_WIDTHS))]
+assert CHUNKS[-1].stop == T
 
 WARM_MATMULS = 10
 
-FLOPS = 2 * (2 * C * C * HALVES * N)
+FLOPS = 2 * (2 * C * C * T)
 
 
 def tile_inter_classifier_kernel(tc, base, xs, w1, b1, w2, b2, offs, out):
     nc = tc.nc
     with (
         tc.tile_pool(name="held", bufs=1) as held,
-        tc.psum_pool(name="psum", bufs=BLOCKS * HALVES) as psum,
+        tc.psum_pool(name="psum", bufs=4) as psum,
     ):
-        xs_sb = [
-            [held.tile([P, N], BF16, name=f"xs_sb{half}_{d}") for d in range(BLOCKS)] for half in range(HALVES)
-        ]
-        w1_sb = [held.tile([P, C], BF16, name=f"w1_sb{d}") for d in range(BLOCKS)]
+        xs_sb = held.tile([P, BLOCKS, T], BF16, name="xs_sb")
+        w1_sb = held.tile([P, BLOCKS, C], BF16, name="w1_sb")
         w2_sb = held.tile([P, BLOCKS, C], BF16, name="w2_sb")
         b1_sb = held.tile([P, BLOCKS], F32, name="b1_sb")
         b2_sb = held.tile([P, BLOCKS], F32, name="b2_sb")
@@ -34,18 +38,17 @@ def tile_inter_classifier_kernel(tc, base, xs, w1, b1, w2, b2, offs, out):
         window = [held.tile([P, S], F32, name=f"window{c}") for c in range(BLOCKS)]
 
         for d in range(BLOCKS):
-            nc.scalar.dma_start(w1_sb[d][:], w1[d * P : (d + 1) * P, :])
+            nc.scalar.dma_start(w1_sb[:, d, :], w1[d * P : (d + 1) * P, :])
         with nc.allow_non_contiguous_dma(reason="one float32 of a bias to each partition"):
             nc.scalar.dma_start(b1_sb[:], b1.rearrange("(k p) o -> p (k o)", p=P))
+            nc.scalar.dma_start(b2_sb[:], b2.rearrange("(c p) o -> p (c o)", p=P))
         for half in range(HALVES):
             for d in range(BLOCKS):
-                nc.sync.dma_start(xs_sb[half][d][:], xs[d * P : (d + 1) * P, half * N : (half + 1) * N])
+                nc.sync.dma_start(xs_sb[:, d, half * N : (half + 1) * N], xs[d * P : (d + 1) * P, half * N : (half + 1) * N])
         nc.sync.dma_start(w2_sb[:], w2.rearrange("(k p) c -> p k c", p=P))
-        with nc.allow_non_contiguous_dma(reason="one float32 of a bias to each partition"):
-            nc.sync.dma_start(b2_sb[:], b2.rearrange("(c p) o -> p (c o)", p=P))
+        nc.sync.dma_start(window[0][:], base[0:P, :])
         nc.sync.dma_start(offsets[:], offs)
-        for c in range(BLOCKS):
-            nc.sync.dma_start(window[c][:], base[c * P : (c + 1) * P, :])
+        nc.sync.dma_start(window[1][:], base[P : 2 * P, :])
 
         zeros = held.tile([P, P], BF16, name="zeros")
         nc.vector.memset(zeros[:], 0.0)
@@ -56,39 +59,37 @@ def tile_inter_classifier_kernel(tc, base, xs, w1, b1, w2, b2, offs, out):
         table_warmer = held.tile([P, 1], F32, name="table_warmer")
         nc.scalar.activation(table_warmer[:], zeros[:, 0:1], RELU)
 
-        h_sb = [[None] * HALVES for k in range(BLOCKS)]
-        for half in range(HALVES):
-            h_ps = [psum.tile([P, N], F32, name=f"h_ps{k}", tag="h_ps") for k in range(BLOCKS)]
+        h_sb = held.tile([P, BLOCKS, T], BF16, name="h_sb")
+        for tokens in CHUNKS:
+            h_ps = [psum.tile([P, tokens.stop - tokens.start], F32, name=f"h_ps{k}", tag="h_ps") for k in range(BLOCKS)]
             for d in range(BLOCKS):
                 for k in range(BLOCKS):
                     nc.tensor.matmul(
                         h_ps[k][:],
-                        w1_sb[d][:, k * P : (k + 1) * P],
-                        xs_sb[half][d][:],
+                        w1_sb[:, d, k * P : (k + 1) * P],
+                        xs_sb[:, d, tokens],
                         start=(d == 0),
                         stop=(d == BLOCKS - 1),
                     )
-            for k in range(BLOCKS):
-                h_sb[k][half] = held.tile([P, N], BF16, name=f"h_sb{k}_{half}")
-                if k == 0:
-                    nc.scalar.activation(h_sb[k][half][:], h_ps[k][:], RELU, bias=b1_sb[:, k : k + 1])
-                else:
-                    nc.vector.tensor_scalar(h_sb[k][half][:], h_ps[k][:], b1_sb[:, k : k + 1], 0.0, ADD, MAX)
+            nc.scalar.activation(h_sb[:, 0, tokens], h_ps[0][:], RELU, bias=b1_sb[:, 0:1])
+            nc.vector.tensor_scalar(h_sb[:, 1, tokens], h_ps[1][:], b1_sb[:, 1:2], 0.0, ADD, MAX)
 
-        y_sb = [[None] * HALVES for c in range(BLOCKS)]
         for c in range(BLOCKS):
-            for half in range(HALVES):
-                y_ps = psum.tile([P, N], F32, name="y_ps")
+            y_sb = held.tile([P, T], F32, name=f"y_sb{c}")
+            for tokens in CHUNKS:
+                y_ps = psum.tile([P, tokens.stop - tokens.start], F32, name="y_ps")
                 for k in range(BLOCKS):
                     nc.tensor.matmul(
                         y_ps[:],
                         w2_sb[:, k, c * P : (c + 1) * P],
-                        h_sb[k][half][:],
+                        h_sb[:, k, tokens],
                         start=(k == 0),
                         stop=(k == BLOCKS - 1),
                     )
-                y_sb[c][half] = held.tile([P, N], F32, name=f"y_sb{c}_{half}")
-                nc.scalar.activation(y_sb[c][half][:], y_ps[:], IDENTITY, bias=b2_sb[:, c : c + 1])
+                if c == 0 and tokens.start == 0:
+                    nc.vector.tensor_scalar(y_sb[:, tokens], y_ps[:], b2_sb[:, c : c + 1], None, ADD)
+                else:
+                    nc.scalar.activation(y_sb[:, tokens], y_ps[:], IDENTITY, bias=b2_sb[:, c : c + 1])
 
-            nc.vector.tensor_tensor(window[c][:].indirect(offsets[:]), y_sb[c][0][:], y_sb[c][1][:], ADD)
+            nc.vector.tensor_tensor(window[c][:].indirect(offsets[:]), y_sb[:, 0:N], y_sb[:, N:T], ADD)
             nc.sync.dma_start(out[c * P : (c + 1) * P, :], window[c][:])

@@ -39,16 +39,17 @@ def tile_inter_classifier_kernel(tc, base, xs, w1, b1, w2, b2, offs, out):
 
         for d in range(BLOCKS):
             nc.scalar.dma_start(w1_sb[:, d, :], w1[d * P : (d + 1) * P, :])
-        with nc.allow_non_contiguous_dma(reason="one float32 of a bias to each partition"):
-            nc.scalar.dma_start(b1_sb[:], b1.rearrange("(k p) o -> p (k o)", p=P))
-            nc.scalar.dma_start(b2_sb[:], b2.rearrange("(c p) o -> p (c o)", p=P))
+        nc.scalar.dma_start(b1_sb[:], b1.rearrange("(p k) o -> p (k o)", k=BLOCKS))
+        nc.scalar.dma_start(b2_sb[:], b2.rearrange("(p c) o -> p (c o)", c=BLOCKS))
         for half in range(HALVES):
             for d in range(BLOCKS):
                 nc.sync.dma_start(xs_sb[:, d, half * N : (half + 1) * N], xs[d * P : (d + 1) * P, half * N : (half + 1) * N])
-        nc.sync.dma_start(w2_sb[:], w2.rearrange("(k p) c -> p k c", p=P))
-        nc.sync.dma_start(window[0][:], base[0:P, :])
+        base_blocks = base.rearrange("(p c) s -> p c s", c=BLOCKS)
+        out_blocks = out.rearrange("(p c) s -> p c s", c=BLOCKS)
+        nc.sync.dma_start(w2_sb[:], w2.rearrange("(p k) c -> p k c", k=BLOCKS))
+        nc.sync.dma_start(window[0][:], base_blocks[:, 0, :])
         nc.sync.dma_start(offsets[:], offs)
-        nc.sync.dma_start(window[1][:], base[P : 2 * P, :])
+        nc.sync.dma_start(window[1][:], base_blocks[:, 1, :])
 
         zeros = held.tile([P, P], BF16, name="zeros")
         nc.vector.memset(zeros[:], 0.0)
@@ -66,7 +67,7 @@ def tile_inter_classifier_kernel(tc, base, xs, w1, b1, w2, b2, offs, out):
                 for k in range(BLOCKS):
                     nc.tensor.matmul(
                         h_ps[k][:],
-                        w1_sb[:, d, k * P : (k + 1) * P],
+                        w1_sb[:, d, k::BLOCKS],
                         xs_sb[:, d, tokens],
                         start=(d == 0),
                         stop=(d == BLOCKS - 1),
@@ -81,7 +82,7 @@ def tile_inter_classifier_kernel(tc, base, xs, w1, b1, w2, b2, offs, out):
                 for k in range(BLOCKS):
                     nc.tensor.matmul(
                         y_ps[:],
-                        w2_sb[:, k, c * P : (c + 1) * P],
+                        w2_sb[:, k, c::BLOCKS],
                         h_sb[:, k, tokens],
                         start=(k == 0),
                         stop=(k == BLOCKS - 1),
@@ -92,4 +93,4 @@ def tile_inter_classifier_kernel(tc, base, xs, w1, b1, w2, b2, offs, out):
                     nc.scalar.activation(y_sb[:, tokens], y_ps[:], IDENTITY, bias=b2_sb[:, c : c + 1])
 
             nc.vector.tensor_tensor(window[c][:].indirect(offsets[:]), y_sb[:, 0:N], y_sb[:, N:T], ADD)
-            nc.sync.dma_start(out[c * P : (c + 1) * P, :], window[c][:])
+            nc.sync.dma_start(out_blocks[:, c, :], window[c][:])

@@ -14,7 +14,7 @@ BLOCKS = C // P
 
 HALVES = 2
 
-CHUNK_WIDTHS = (384, 192, 192)
+CHUNK_WIDTHS = (384, 384)
 CHUNKS = [slice(sum(CHUNK_WIDTHS[:i]), sum(CHUNK_WIDTHS[: i + 1])) for i in range(len(CHUNK_WIDTHS))]
 assert CHUNKS[-1].stop == T
 

@@ -12,13 +12,12 @@ N = 384
 T = 2 * N
 BLOCKS = C // P
 
-HALVES = 2
 
-CHUNK_WIDTHS = (384, 384)
+CHUNK_WIDTHS = (256, 256, 256)
 CHUNKS = [slice(sum(CHUNK_WIDTHS[:i]), sum(CHUNK_WIDTHS[: i + 1])) for i in range(len(CHUNK_WIDTHS))]
 assert CHUNKS[-1].stop == T
 
-WARM_MATMULS = 10
+WARM_MATMULS = 9
 
 FLOPS = 2 * (2 * C * C * T)
 
@@ -41,9 +40,10 @@ def tile_inter_classifier_kernel(tc, base, xs, w1, b1, w2, b2, offs, out):
             nc.scalar.dma_start(w1_sb[:, d, :], w1[d * P : (d + 1) * P, :])
         nc.scalar.dma_start(b1_sb[:], b1.rearrange("(p k) o -> p (k o)", k=BLOCKS))
         nc.scalar.dma_start(b2_sb[:], b2.rearrange("(p c) o -> p (c o)", c=BLOCKS))
-        for half in range(HALVES):
-            for d in range(BLOCKS):
-                nc.sync.dma_start(xs_sb[:, d, half * N : (half + 1) * N], xs[d * P : (d + 1) * P, half * N : (half + 1) * N])
+        for d in range(BLOCKS):
+            nc.sync.dma_start(xs_sb[:, d, CHUNKS[0]], xs[d * P : (d + 1) * P, CHUNKS[0]])
+        for tokens in CHUNKS[1:]:
+            nc.sync.dma_start(xs_sb[:, :, tokens], xs.rearrange("(d p) t -> p d t", p=P)[:, :, tokens])
         base_blocks = base.rearrange("(p c) s -> p c s", c=BLOCKS)
         out_blocks = out.rearrange("(p c) s -> p c s", c=BLOCKS)
         nc.sync.dma_start(w2_sb[:], w2.rearrange("(p k) c -> p k c", k=BLOCKS))

import concourse.mybir as mybir

BF16, F32, U16 = mybir.dt.bfloat16, mybir.dt.float32, mybir.dt.uint16
ADD, MAX = mybir.AluOpType.add, mybir.AluOpType.max
RELU = mybir.ActivationFunctionType.Relu
IDENTITY = mybir.ActivationFunctionType.Identity

P = 128
C = 256
S = 768
N = 384
T = 2 * N
BLOCKS = C // P


CHUNK_WIDTHS = (256, 256, 256)
CHUNKS = [slice(sum(CHUNK_WIDTHS[:i]), sum(CHUNK_WIDTHS[: i + 1])) for i in range(len(CHUNK_WIDTHS))]
assert CHUNKS[-1].stop == T

WARM_MATMULS = 9

FLOPS = 2 * (2 * C * C * T)


def tile_inter_classifier_kernel(tc, base, xs, w1, b1, w2, b2, offs, out):
    nc = tc.nc
    with (
        tc.tile_pool(name="held", bufs=1) as held,
        tc.psum_pool(name="psum", bufs=4) as psum,
    ):
        xs_sb = held.tile([P, BLOCKS, T], BF16, name="xs_sb")
        w1_sb = held.tile([P, BLOCKS, C], BF16, name="w1_sb")
        w2_sb = held.tile([P, BLOCKS, C], BF16, name="w2_sb")
        b1_sb = held.tile([P, BLOCKS], F32, name="b1_sb")
        b2_sb = held.tile([P, BLOCKS], F32, name="b2_sb")
        offsets = held.tile([P, N // 16], U16, name="offsets")
        window = [held.tile([P, S], F32, name=f"window{c}") for c in range(BLOCKS)]

        for d in range(BLOCKS):
            nc.scalar.dma_start(w1_sb[:, d, :], w1[d * P : (d + 1) * P, :])
        nc.scalar.dma_start(b1_sb[:], b1.rearrange("(p k) o -> p (k o)", k=BLOCKS))
        nc.scalar.dma_start(b2_sb[:], b2.rearrange("(p c) o -> p (c o)", c=BLOCKS))
        for d in range(BLOCKS):
            nc.sync.dma_start(xs_sb[:, d, CHUNKS[0]], xs[d * P : (d + 1) * P, CHUNKS[0]])
        for tokens in CHUNKS[1:]:
            nc.sync.dma_start(xs_sb[:, :, tokens], xs.rearrange("(d p) t -> p d t", p=P)[:, :, tokens])
        base_blocks = base.rearrange("(p c) s -> p c s", c=BLOCKS)
        out_blocks = out.rearrange("(p c) s -> p c s", c=BLOCKS)
        nc.sync.dma_start(w2_sb[:], w2.rearrange("(p k) c -> p k c", k=BLOCKS))
        nc.sync.dma_start(window[0][:], base_blocks[:, 0, :])
        nc.sync.dma_start(offsets[:], offs)
        nc.sync.dma_start(window[1][:], base_blocks[:, 1, :])

        zeros = held.tile([P, P], BF16, name="zeros")
        nc.vector.memset(zeros[:], 0.0)
        warm_ps = psum.tile([P, P], F32, name="warm_ps", tag="y_ps")
        for i in range(WARM_MATMULS):
            nc.tensor.matmul(warm_ps[:], zeros[:], zeros[:], start=True, stop=True)

        table_warmer = held.tile([P, 1], F32, name="table_warmer")
        nc.scalar.activation(table_warmer[:], zeros[:, 0:1], RELU)

        h_sb = held.tile([P, BLOCKS, T], BF16, name="h_sb")
        for tokens in CHUNKS:
            h_ps = [psum.tile([P, tokens.stop - tokens.start], F32, name=f"h_ps{k}", tag="h_ps") for k in range(BLOCKS)]
            for d in range(BLOCKS):
                for k in range(BLOCKS):
                    nc.tensor.matmul(
                        h_ps[k][:],
                        w1_sb[:, d, k::BLOCKS],
                        xs_sb[:, d, tokens],
                        start=(d == 0),
                        stop=(d == BLOCKS - 1),
                    )
            nc.scalar.activation(h_sb[:, 0, tokens], h_ps[0][:], RELU, bias=b1_sb[:, 0:1])
            nc.vector.tensor_scalar(h_sb[:, 1, tokens], h_ps[1][:], b1_sb[:, 1:2], 0.0, ADD, MAX)

        for c in range(BLOCKS):
            y_sb = held.tile([P, T], F32, name=f"y_sb{c}")
            for tokens in CHUNKS:
                y_ps = psum.tile([P, tokens.stop - tokens.start], F32, name="y_ps")
                for k in range(BLOCKS):
                    nc.tensor.matmul(
                        y_ps[:],
                        w2_sb[:, k, c::BLOCKS],
                        h_sb[:, k, tokens],
                        start=(k == 0),
                        stop=(k == BLOCKS - 1),
                    )
                if c == 0 and tokens.start == 0:
                    nc.vector.tensor_scalar(y_sb[:, tokens], y_ps[:], b2_sb[:, c : c + 1], None, ADD)
                else:
                    nc.scalar.activation(y_sb[:, tokens], y_ps[:], IDENTITY, bias=b2_sb[:, c : c + 1])

            nc.vector.tensor_tensor(window[c][:].indirect(offsets[:]), y_sb[:, 0:N], y_sb[:, N:T], ADD)
            nc.sync.dma_start(out_blocks[:, c, :], window[c][:])
